import numpy as np
import ml_dtypes


def mxq(x, axis, fmt="e4m3"):
    dtype, down = {"e4m3": (ml_dtypes.float8_e4m3fn, 7), "e5m2": (ml_dtypes.float8_e5m2, 14)}[fmt]
    v = np.moveaxis(np.asarray(x, np.float32).astype(ml_dtypes.bfloat16).astype(np.float64), axis, -1)
    blocks = v.reshape(v.shape[:-1] + (-1, 32))
    amax = np.abs(blocks).max(-1, keepdims=True)
    byte = np.maximum(np.where(amax > 0, np.frexp(amax)[1] - 1 + 127, 0) - down, 1)
    scale = np.exp2(byte - 127.0)
    codes = (blocks / scale).astype(np.float32).astype(dtype).astype(np.float64)
    return np.moveaxis((codes * scale).reshape(v.shape), -1, axis)


WIDE = False


def mx_kscale(k):
    if not WIDE:
        return np.ones(k)
    levels = np.array([10, -10, 5, -5, 0])
    a = np.random.permutation(np.resize(levels, k // 512 * 4)).reshape(k // 512, 4)
    idx = np.arange(k)
    return np.exp2(a[idx // 512, idx % 128 // 32])


BF16 = ml_dtypes.bfloat16


def bf(x):
    return np.asarray(x, np.float32).astype(BF16)


def f64(x):
    return np.asarray(x).astype(np.float64)


B, L, D, F, K = 256, 8, 512, 1024, 16
EPS = 1e-12


def silu(v):
    return v / (1.0 + np.exp(-v))


def l2norm(t, axis):
    n = np.sqrt((t * t).sum(axis=axis, keepdims=True))
    return t / np.maximum(n, EPS)


def mix_draw(rows, cols):
    return np.random.standard_normal((L, rows, cols)) * np.sqrt(np.e / K) * np.exp(0.5 * np.random.standard_normal((L, 1, cols)))


def hidden_draw():
    return silu(3.0 * np.random.standard_normal((B, L, F))) * np.random.standard_normal((B, L, F)) * 3.0 / np.sqrt(D)


def setup_inputs():
    t = mx_kscale(F)
    g = np.sqrt(np.mean(1.0 / t**2))
    return {"h": bf(hidden_draw() * t * g),
            "w_down_mix": bf(mix_draw(F, D) / t[:, None])}


def reference(h, w_down_mix):
    wd = l2norm(f64(w_down_mix), 1)
    y = mxq(f64(h).transpose(1, 0, 2), 2, "e4m3") @ mxq(wd, 1, "e4m3")
    return l2norm(y, -1).transpose(1, 0, 2)

@@ -1,0 +1,184 @@
+from contextlib import ExitStack
+
+import concourse.mybir as mybir
+from concourse.masks import make_identity
+
+BF16 = mybir.dt.bfloat16
+F32 = mybir.dt.float32
+U32 = mybir.dt.uint32
+U8 = mybir.dt.uint8
+FP8X4 = mybir.dt.float8_e4m3fn_x4
+ACT = mybir.ActivationFunctionType
+ALU = mybir.AluOpType
+
+P = 128
+PACK = 4
+BATCH, TOKENS, HIDDEN, OUT = 256, 8, 1024, 512
+PASSES = HIDDEN // (P * PACK)
+ROWS = PASSES * PACK
+HALVES = 2
+B_TILES = BATCH // P
+J_BLOCKS = OUT // P
+EPS = 1e-12
+TOKENS_PER_H_LOAD = 2
+
+FLOPS = 2 * BATCH * TOKENS * HIDDEN * OUT
+
+
+def tile_npertokenswishglu_basis_pb_kernel(tc, h, w_down_mix, out):
+    nc = tc.nc
+    with ExitStack() as stack:
+        const = stack.enter_context(tc.tile_pool(name="const", bufs=1))
+        w_pool = stack.enter_context(tc.tile_pool(name="w_pool", bufs=TOKENS))
+        h_pool = stack.enter_context(tc.tile_pool(name="h_pool", bufs=TOKENS // TOKENS_PER_H_LOAD))
+        h_mx = stack.enter_context(tc.tile_pool(name="h_mx", bufs=TOKENS))
+        work = stack.enter_context(tc.tile_pool(name="work", bufs=2))
+        unread = stack.enter_context(tc.tile_pool(name="unread", bufs=4))
+        small = stack.enter_context(tc.tile_pool(name="small", bufs=4))
+        result = stack.enter_context(tc.tile_pool(name="result", bufs=3))
+        wT_psum = stack.enter_context(tc.psum_pool(name="wT_psum", bufs=3))
+        inv_psum = stack.enter_context(tc.psum_pool(name="inv_psum", bufs=2))
+        hT_psum = stack.enter_context(tc.psum_pool(name="hT_psum", bufs=1))
+        y_psum = stack.enter_context(tc.psum_pool(name="y_psum", bufs=2))
+
+        w_sb = []
+        h_sb = []
+        h_view = h.rearrange("(i p) l f -> p i l f", p=P)
+        for l in range(TOKENS):
+            w_tile = w_pool.tile([P, ROWS, OUT], BF16, name="w_tile")
+            nc.sync.dma_start(
+                out=w_tile[:].rearrange("p (g e) j -> p g (e j)", e=2),
+                in_=w_down_mix[l].rearrange("(g p e) j -> p g (e j)", p=P, e=2),
+            )
+            w_sb.append(w_tile)
+            if l < TOKENS // TOKENS_PER_H_LOAD:
+                h_tile = h_pool.tile([P, B_TILES, TOKENS_PER_H_LOAD, HIDDEN], BF16, name="h_tile")
+                first = l * TOKENS_PER_H_LOAD
+                nc.sync.dma_start(out=h_tile[:], in_=h_view[:, :, first : first + TOKENS_PER_H_LOAD, :])
+                h_sb.append(h_tile)
+
+        ident_bf = const.tile([P, P], BF16, name="ident_bf")
+        make_identity(nc, ident_bf[:])
+        ident_f32 = const.tile([P, P], F32, name="ident_f32")
+        make_identity(nc, ident_f32[:])
+
+        one = const.tile([P, 1], F32, name="one")
+        nc.vector.memset(one[:], 1.0)
+        nc.scalar.activation(out=one[:], in_=one[:], func=ACT.Sqrt)
+
+        def inverse_norm(sum_sq, width, name):
+            clamped = small.tile([P, width], F32, name=name + "_clamped")
+            nc.vector.tensor_scalar_max(out=clamped[:], in0=sum_sq[:], scalar1=EPS * EPS)
+            recip = small.tile([P, width], F32, name=name + "_recip")
+            nc.vector.reciprocal(out=recip[:], in_=clamped[:])
+            inv = small.tile([P, width], F32, name=name + "_inv")
+            nc.scalar.activation(out=inv[:], in_=recip[:], func=ACT.Sqrt)
+            return inv
+
+        def weight_norms(l):
+            col_sq = small.tile([P, J_BLOCKS], F32, name="col_sq")
+            for m in range(J_BLOCKS):
+                wT = wT_psum.tile([P, ROWS, P], BF16, name="wT")
+                for r in range(ROWS):
+                    nc.tensor.transpose(wT[:, r, :], w_sb[l][:, r, m * P : (m + 1) * P], ident_bf[:])
+                squares = unread.tile([P, ROWS * P], BF16, name="squares")
+                nc.scalar.activation(
+                    out=squares[:],
+                    in_=wT[:].rearrange("p r f -> p (r f)"),
+                    func=ACT.Square,
+                    accum_out=col_sq[:, m : m + 1],
+                )
+            col_inv = inverse_norm(col_sq, J_BLOCKS, "col")
+            inv_rows = inv_psum.tile([P, OUT], F32, name="inv_rows")
+            for m in range(J_BLOCKS):
+                nc.tensor.matmul(
+                    out=inv_rows[:, m * P : (m + 1) * P],
+                    lhsT=col_inv[:, m : m + 1].to_broadcast([P, P]),
+                    rhs=ident_f32[:],
+                    start=True,
+                    stop=True,
+                )
+            return inv_rows
+
+        def quantise_weight(l, inv_rows):
+            nd = work.tile([P, PASSES, OUT, PACK], BF16, name="nd", align_bytes=64)
+            codes = work.tile([P, PASSES, OUT], U32, name="w_codes", align_bytes=64)
+            scales = work.tile([P, PASSES, OUT], U8, name="w_scales", align_bytes=64)
+            for c in range(PASSES):
+                nc.vector.tensor_tensor(
+                    out=nd[:, c],
+                    in0=w_sb[l][:, c * PACK : (c + 1) * PACK, :].rearrange("p t j -> p j t"),
+                    in1=inv_rows[:].unsqueeze(2).to_broadcast([P, OUT, PACK]),
+                    op=ALU.mult,
+                )
+            for c in range(PASSES):
+                nc.vector.quantize_mx(
+                    out=codes[:, c, :].bitcast(FP8X4),
+                    scales=scales[:, c, :],
+                    in_=nd[:, c].rearrange("p j t -> p (j t)"),
+                )
+            return codes, scales
+
+        def quantise_hidden(l):
+            h_tile = h_sb[l // TOKENS_PER_H_LOAD]
+            grouped = work.tile([P, PASSES * BATCH * PACK], BF16, name="h_grouped", align_bytes=64)
+            grouped_words = grouped[:].bitcast(F32).rearrange("p (c b u) -> p c b u", c=PASSES, u=HALVES)
+            for c in range(PASSES):
+                hT = hT_psum.tile([P, HALVES, B_TILES, P], F32, name="hT")
+                for u in range(HALVES):
+                    for i in range(B_TILES):
+                        words = h_tile[:, i, l % TOKENS_PER_H_LOAD, :].bitcast(F32)
+                        first = (c * HALVES + u) * P
+                        nc.tensor.transpose(hT[:, u, i, :], words[:, first : first + P], ident_f32[:])
+                nc.vector.tensor_copy(out=grouped_words[:, c], in_=hT[:].rearrange("p u i b -> p (i b) u"))
+            codes = h_mx.tile([P, PASSES * BATCH], U32, name="h_codes", align_bytes=64)
+            scales = h_mx.tile([P, PASSES * BATCH], U8, name="h_scales", align_bytes=64)
+            nc.vector.quantize_mx(out=codes[:].bitcast(FP8X4), scales=scales[:], in_=grouped[:])
+            return codes, scales
+
+        def project(l, h_q, w_q):
+            h_codes, h_scales = h_q
+            w_codes, w_scales = w_q
+            row_sq = small.tile([P, B_TILES], F32, name="row_sq")
+            y_tiles = []
+            for i in range(B_TILES):
+                y = y_psum.tile([P, OUT], F32, name="y")
+                for c in range(PASSES):
+                    b_cols = slice((c * B_TILES + i) * P, (c * B_TILES + i + 1) * P)
+                    nc.tensor.matmul_mx(
+                        out=y[:],
+                        lhsT=h_codes[:, b_cols].bitcast(FP8X4),
+                        lhsT_scale=h_scales[:, b_cols],
+                        rhs=w_codes[:, c, :].bitcast(FP8X4),
+                        rhs_scale=w_scales[:, c, :],
+                        start=(c == 0),
+                        stop=(c == PASSES - 1),
+                    )
+                y_squares = unread.tile([P, OUT], BF16, name="y_squares")
+                nc.scalar.activation(
+                    out=y_squares[:], in_=y[:], func=ACT.Square, accum_out=row_sq[:, i : i + 1]
+                )
+                y_tiles.append(y)
+            row_inv = inverse_norm(row_sq, B_TILES, "row")
+            unit = result.tile([P, B_TILES, OUT], F32, name="unit")
+            for i in range(B_TILES):
+                nc.scalar.activation(
+                    out=unit[:, i, :], in_=y_tiles[i][:], func=ACT.Copy, scale=row_inv[:, i : i + 1]
+                )
+            nc.sync.dma_start(out=out.rearrange("(i p) l j -> p i l j", p=P)[:, :, l, :], in_=unit[:])
+
+        NORMS_AHEAD = 1
+        HIDDEN_AHEAD = 2
+        inv_rows = {}
+        h_q = {}
+        for l in range(NORMS_AHEAD):
+            inv_rows[l] = weight_norms(l)
+        for l in range(HIDDEN_AHEAD):
+            h_q[l] = quantise_hidden(l)
+        for l in range(TOKENS):
+            if l + NORMS_AHEAD < TOKENS:
+                inv_rows[l + NORMS_AHEAD] = weight_norms(l + NORMS_AHEAD)
+            if l + HIDDEN_AHEAD < TOKENS:
+                h_q[l + HIDDEN_AHEAD] = quantise_hidden(l + HIDDEN_AHEAD)
+            w_q = quantise_weight(l, inv_rows[l])
+            project(l, h_q[l], w_q)

@@ -18,7 +18,7 @@ PASSES = HIDDEN // (P * PACK)
 ROWS = PASSES * PACK
 HALVES = 2
 B_TILES = BATCH // P
-J_BLOCKS = OUT // P
+J_HALVES = OUT // (2 * P)
 EPS = 1e-12
 TOKENS_PER_H_LOAD = 2
 
@@ -57,8 +57,6 @@ def tile_npertokenswishglu_basis_pb_kernel(tc, h, w_down_mix, out):
                 nc.sync.dma_start(out=h_tile[:], in_=h_view[:, :, first : first + TOKENS_PER_H_LOAD, :])
                 h_sb.append(h_tile)
 
-        ident_bf = const.tile([P, P], BF16, name="ident_bf")
-        make_identity(nc, ident_bf[:])
         ident_f32 = const.tile([P, P], F32, name="ident_f32")
         make_identity(nc, ident_f32[:])
 
@@ -68,7 +66,7 @@ def tile_npertokenswishglu_basis_pb_kernel(tc, h, w_down_mix, out):
 
         def inverse_norm(sum_sq, width, name):
             clamped = small.tile([P, width], F32, name=name + "_clamped")
-            nc.vector.tensor_scalar_max(out=clamped[:], in0=sum_sq[:], scalar1=EPS * EPS)
+            nc.vector.tensor_scalar_max(out=clamped[:], in0=sum_sq, scalar1=EPS * EPS)
             recip = small.tile([P, width], F32, name=name + "_recip")
             nc.vector.reciprocal(out=recip[:], in_=clamped[:])
             inv = small.tile([P, width], F32, name=name + "_inv")
@@ -76,28 +74,40 @@ def tile_npertokenswishglu_basis_pb_kernel(tc, h, w_down_mix, out):
             return inv
 
         def weight_norms(l):
-            col_sq = small.tile([P, J_BLOCKS], F32, name="col_sq")
-            for m in range(J_BLOCKS):
-                wT = wT_psum.tile([P, ROWS, P], BF16, name="wT")
-                for r in range(ROWS):
-                    nc.tensor.transpose(wT[:, r, :], w_sb[l][:, r, m * P : (m + 1) * P], ident_bf[:])
-                squares = unread.tile([P, ROWS * P], BF16, name="squares")
-                nc.scalar.activation(
-                    out=squares[:],
-                    in_=wT[:].rearrange("p r f -> p (r f)"),
-                    func=ACT.Square,
-                    accum_out=col_sq[:, m : m + 1],
-                )
-            col_inv = inverse_norm(col_sq, J_BLOCKS, "col")
-            inv_rows = inv_psum.tile([P, OUT], F32, name="inv_rows")
-            for m in range(J_BLOCKS):
-                nc.tensor.matmul(
-                    out=inv_rows[:, m * P : (m + 1) * P],
-                    lhsT=col_inv[:, m : m + 1].to_broadcast([P, P]),
-                    rhs=ident_f32[:],
-                    start=True,
-                    stop=True,
-                )
+            part_sq = small.tile([P, PASSES, J_HALVES, 2], F32, name="part_sq")
+            for a in range(J_HALVES):
+                for c in range(PASSES):
+                    wT = wT_psum.tile([P, PACK * P], F32, name="wT")
+                    for t in range(PACK):
+                        words = w_sb[l][:, c * PACK + t, :].bitcast(F32)
+                        nc.tensor.transpose(
+                            wT[:, t * P : (t + 1) * P], words[:, a * P : (a + 1) * P], ident_f32[:]
+                        )
+                    pairs = wT[:].bitcast(BF16).rearrange("p (n e) -> p e n", e=2)
+                    for e in range(2):
+                        squares = unread.tile([P, PACK * P], BF16, name="squares")
+                        nc.scalar.activation(
+                            out=squares[:],
+                            in_=pairs[:, e, :],
+                            func=ACT.Square,
+                            accum_out=part_sq[:, c, a, e : e + 1],
+                        )
+            col_sq = small.tile([P, J_HALVES, 2], F32, name="col_sq")
+            nc.vector.tensor_tensor(out=col_sq[:], in0=part_sq[:, 0], in1=part_sq[:, 1], op=ALU.add)
+            col_inv = inverse_norm(col_sq[:].rearrange("p a e -> p (a e)"), J_HALVES * 2, "col")
+            repeated = work.tile([P, J_HALVES * 2, P], F32, name="repeated")
+            nc.gpsimd.tensor_scalar(
+                out=repeated[:],
+                in0=col_inv[:].unsqueeze(2).to_broadcast([P, J_HALVES * 2, P]),
+                scalar1=1.0,
+                scalar2=0.0,
+                op0=ALU.mult,
+                op1=ALU.add,
+            )
+            inv_rows = inv_psum.tile([P, J_HALVES, 2, P], F32, name="inv_rows")
+            for a in range(J_HALVES):
+                for e in range(2):
+                    nc.tensor.transpose(inv_rows[:, a, e, :], repeated[:, a * 2 + e, :], ident_f32[:])
             return inv_rows
 
         def quantise_weight(l, inv_rows):
@@ -105,12 +115,16 @@ def tile_npertokenswishglu_basis_pb_kernel(tc, h, w_down_mix, out):
             codes = work.tile([P, PASSES, OUT], U32, name="w_codes", align_bytes=64)
             scales = work.tile([P, PASSES, OUT], U8, name="w_scales", align_bytes=64)
             for c in range(PASSES):
-                nc.vector.tensor_tensor(
-                    out=nd[:, c],
-                    in0=w_sb[l][:, c * PACK : (c + 1) * PACK, :].rearrange("p t j -> p j t"),
-                    in1=inv_rows[:].unsqueeze(2).to_broadcast([P, OUT, PACK]),
-                    op=ALU.mult,
-                )
+                for a in range(J_HALVES):
+                    j_cols = slice(a * 2 * P, (a + 1) * 2 * P)
+                    nc.vector.tensor_tensor(
+                        out=nd[:, c, j_cols, :].rearrange("p (q e) t -> p q e t", e=2),
+                        in0=w_sb[l][:, c * PACK : (c + 1) * PACK, j_cols].rearrange(
+                            "p t (q e) -> p q e t", e=2
+                        ),
+                        in1=inv_rows[:, a].rearrange("p e q -> p q e").unsqueeze(3).to_broadcast([P, P, 2, PACK]),
+                        op=ALU.mult,
+                    )
             for c in range(PASSES):
                 nc.vector.quantize_mx(
                     out=codes[:, c, :].bitcast(FP8X4),
@@ -159,7 +173,7 @@ def tile_npertokenswishglu_basis_pb_kernel(tc, h, w_down_mix, out):
                     out=y_squares[:], in_=y[:], func=ACT.Square, accum_out=row_sq[:, i : i + 1]
                 )
                 y_tiles.append(y)
-            row_inv = inverse_norm(row_sq, B_TILES, "row")
+            row_inv = inverse_norm(row_sq[:], B_TILES, "row")
             unit = result.tile([P, B_TILES, OUT], F32, name="unit")
             for i in range(B_TILES):
                 nc.scalar.activation(

@@ -18,9 +18,10 @@ PASSES = HIDDEN // (P * PACK)
 ROWS = PASSES * PACK
 HALVES = 2
 B_TILES = BATCH // P
-J_HALVES = OUT // (2 * P)
+J_BLOCKS = OUT // P
 EPS = 1e-12
 TOKENS_PER_H_LOAD = 2
+RUN = 4
 
 FLOPS = 2 * BATCH * TOKENS * HIDDEN * OUT
 
@@ -57,6 +58,8 @@ def tile_npertokenswishglu_basis_pb_kernel(tc, h, w_down_mix, out):
                 nc.sync.dma_start(out=h_tile[:], in_=h_view[:, :, first : first + TOKENS_PER_H_LOAD, :])
                 h_sb.append(h_tile)
 
+        ident_bf = const.tile([P, P], BF16, name="ident_bf")
+        make_identity(nc, ident_bf[:])
         ident_f32 = const.tile([P, P], F32, name="ident_f32")
         make_identity(nc, ident_f32[:])
 
@@ -66,7 +69,7 @@ def tile_npertokenswishglu_basis_pb_kernel(tc, h, w_down_mix, out):
 
         def inverse_norm(sum_sq, width, name):
             clamped = small.tile([P, width], F32, name=name + "_clamped")
-            nc.vector.tensor_scalar_max(out=clamped[:], in0=sum_sq, scalar1=EPS * EPS)
+            nc.vector.tensor_scalar_max(out=clamped[:], in0=sum_sq[:], scalar1=EPS * EPS)
             recip = small.tile([P, width], F32, name=name + "_recip")
             nc.vector.reciprocal(out=recip[:], in_=clamped[:])
             inv = small.tile([P, width], F32, name=name + "_inv")
@@ -74,40 +77,28 @@ def tile_npertokenswishglu_basis_pb_kernel(tc, h, w_down_mix, out):
             return inv
 
         def weight_norms(l):
-            part_sq = small.tile([P, PASSES, J_HALVES, 2], F32, name="part_sq")
-            for a in range(J_HALVES):
-                for c in range(PASSES):
-                    wT = wT_psum.tile([P, PACK * P], F32, name="wT")
-                    for t in range(PACK):
-                        words = w_sb[l][:, c * PACK + t, :].bitcast(F32)
-                        nc.tensor.transpose(
-                            wT[:, t * P : (t + 1) * P], words[:, a * P : (a + 1) * P], ident_f32[:]
-                        )
-                    pairs = wT[:].bitcast(BF16).rearrange("p (n e) -> p e n", e=2)
-                    for e in range(2):
-                        squares = unread.tile([P, PACK * P], BF16, name="squares")
-                        nc.scalar.activation(
-                            out=squares[:],
-                            in_=pairs[:, e, :],
-                            func=ACT.Square,
-                            accum_out=part_sq[:, c, a, e : e + 1],
-                        )
-            col_sq = small.tile([P, J_HALVES, 2], F32, name="col_sq")
-            nc.vector.tensor_tensor(out=col_sq[:], in0=part_sq[:, 0], in1=part_sq[:, 1], op=ALU.add)
-            col_inv = inverse_norm(col_sq[:].rearrange("p a e -> p (a e)"), J_HALVES * 2, "col")
-            repeated = work.tile([P, J_HALVES * 2, P], F32, name="repeated")
-            nc.gpsimd.tensor_scalar(
-                out=repeated[:],
-                in0=col_inv[:].unsqueeze(2).to_broadcast([P, J_HALVES * 2, P]),
-                scalar1=1.0,
-                scalar2=0.0,
-                op0=ALU.mult,
-                op1=ALU.add,
-            )
-            inv_rows = inv_psum.tile([P, J_HALVES, 2, P], F32, name="inv_rows")
-            for a in range(J_HALVES):
-                for e in range(2):
-                    nc.tensor.transpose(inv_rows[:, a, e, :], repeated[:, a * 2 + e, :], ident_f32[:])
+            col_sq = small.tile([P, J_BLOCKS], F32, name="col_sq")
+            for m in range(J_BLOCKS):
+                wT = wT_psum.tile([P, ROWS, P], BF16, name="wT")
+                for r in range(ROWS):
+                    nc.tensor.transpose(wT[:, r, :], w_sb[l][:, r, m * P : (m + 1) * P], ident_bf[:])
+                squares = unread.tile([P, ROWS * P], BF16, name="squares")
+                nc.scalar.activation(
+                    out=squares[:],
+                    in_=wT[:].rearrange("p r f -> p (r f)"),
+                    func=ACT.Square,
+                    accum_out=col_sq[:, m : m + 1],
+                )
+            col_inv = inverse_norm(col_sq, J_BLOCKS, "col")
+            inv_rows = inv_psum.tile([P, OUT], F32, name="inv_rows")
+            for m in range(J_BLOCKS):
+                nc.tensor.matmul(
+                    out=inv_rows[:, m * P : (m + 1) * P],
+                    lhsT=col_inv[:, m : m + 1].to_broadcast([P, P]),
+                    rhs=ident_f32[:],
+                    start=True,
+                    stop=True,
+                )
             return inv_rows
 
         def quantise_weight(l, inv_rows):
@@ -115,16 +106,15 @@ def tile_npertokenswishglu_basis_pb_kernel(tc, h, w_down_mix, out):
             codes = work.tile([P, PASSES, OUT], U32, name="w_codes", align_bytes=64)
             scales = work.tile([P, PASSES, OUT], U8, name="w_scales", align_bytes=64)
             for c in range(PASSES):
-                for a in range(J_HALVES):
-                    j_cols = slice(a * 2 * P, (a + 1) * 2 * P)
-                    nc.vector.tensor_tensor(
-                        out=nd[:, c, j_cols, :].rearrange("p (q e) t -> p q e t", e=2),
-                        in0=w_sb[l][:, c * PACK : (c + 1) * PACK, j_cols].rearrange(
-                            "p t (q e) -> p q e t", e=2
-                        ),
-                        in1=inv_rows[:, a].rearrange("p e q -> p q e").unsqueeze(3).to_broadcast([P, P, 2, PACK]),
-                        op=ALU.mult,
-                    )
+                nc.vector.tensor_tensor(
+                    out=nd[:, c].rearrange("p (n i) t -> p n t i", i=RUN),
+                    in0=w_sb[l][:, c * PACK : (c + 1) * PACK, :].rearrange("p t (n i) -> p n t i", i=RUN),
+                    in1=inv_rows[:]
+                    .rearrange("p (n i) -> p n i", i=RUN)
+                    .unsqueeze(2)
+                    .to_broadcast([P, OUT // RUN, PACK, RUN]),
+                    op=ALU.mult,
+                )
             for c in range(PASSES):
                 nc.vector.quantize_mx(
                     out=codes[:, c, :].bitcast(FP8X4),
@@ -173,7 +163,7 @@ def tile_npertokenswishglu_basis_pb_kernel(tc, h, w_down_mix, out):
                     out=y_squares[:], in_=y[:], func=ACT.Square, accum_out=row_sq[:, i : i + 1]
                 )
                 y_tiles.append(y)
-            row_inv = inverse_norm(row_sq[:], B_TILES, "row")
+            row_inv = inverse_norm(row_sq, B_TILES, "row")
             unit = result.tile([P, B_TILES, OUT], F32, name="unit")
             for i in range(B_TILES):
                 nc.scalar.activation(

@@ -21,6 +21,7 @@ B_TILES = BATCH // P
 J_BLOCKS = OUT // P
 EPS = 1e-12
 TOKENS_PER_H_LOAD = 2
+VECTOR_COLS = 320
 RUN = 4
 
 FLOPS = 2 * BATCH * TOKENS * HIDDEN * OUT
@@ -65,15 +66,13 @@ def tile_npertokenswishglu_basis_pb_kernel(tc, h, w_down_mix, out):
 
         one = const.tile([P, 1], F32, name="one")
         nc.vector.memset(one[:], 1.0)
-        nc.scalar.activation(out=one[:], in_=one[:], func=ACT.Sqrt)
+        nc.scalar.activation(out=one[:], in_=one[:], func=ACT.Abs_reciprocal_sqrt)
 
         def inverse_norm(sum_sq, width, name):
-            clamped = small.tile([P, width], F32, name=name + "_clamped")
-            nc.vector.tensor_scalar_max(out=clamped[:], in0=sum_sq[:], scalar1=EPS * EPS)
-            recip = small.tile([P, width], F32, name=name + "_recip")
-            nc.vector.reciprocal(out=recip[:], in_=clamped[:])
+            excess = small.tile([P, width], F32, name=name + "_excess")
+            nc.scalar.activation(out=excess[:], in_=sum_sq[:], func=ACT.Relu, bias=-EPS * EPS)
             inv = small.tile([P, width], F32, name=name + "_inv")
-            nc.scalar.activation(out=inv[:], in_=recip[:], func=ACT.Sqrt)
+            nc.scalar.activation(out=inv[:], in_=excess[:], func=ACT.Abs_reciprocal_sqrt, bias=EPS * EPS)
             return inv
 
         def weight_norms(l):
@@ -101,20 +100,25 @@ def tile_npertokenswishglu_basis_pb_kernel(tc, h, w_down_mix, out):
                 )
             return inv_rows
 
+        def scale_columns(engine, l, c, first, last, inv, nd):
+            engine.tensor_tensor(
+                out=nd[:, c, first:last, :].rearrange("p (n i) t -> p n t i", i=RUN),
+                in0=w_sb[l][:, c * PACK : (c + 1) * PACK, first:last].rearrange("p t (n i) -> p n t i", i=RUN),
+                in1=inv.rearrange("p (n i) -> p n i", i=RUN)
+                .unsqueeze(2)
+                .to_broadcast([P, (last - first) // RUN, PACK, RUN]),
+                op=ALU.mult,
+            )
+
         def quantise_weight(l, inv_rows):
             nd = work.tile([P, PASSES, OUT, PACK], BF16, name="nd", align_bytes=64)
             codes = work.tile([P, PASSES, OUT], U32, name="w_codes", align_bytes=64)
             scales = work.tile([P, PASSES, OUT], U8, name="w_scales", align_bytes=64)
+            inv_gpsimd = work.tile([P, OUT - VECTOR_COLS], F32, name="inv_gpsimd")
+            nc.vector.tensor_copy(out=inv_gpsimd[:], in_=inv_rows[:, VECTOR_COLS:])
             for c in range(PASSES):
-                nc.vector.tensor_tensor(
-                    out=nd[:, c].rearrange("p (n i) t -> p n t i", i=RUN),
-                    in0=w_sb[l][:, c * PACK : (c + 1) * PACK, :].rearrange("p t (n i) -> p n t i", i=RUN),
-                    in1=inv_rows[:]
-                    .rearrange("p (n i) -> p n i", i=RUN)
-                    .unsqueeze(2)
-                    .to_broadcast([P, OUT // RUN, PACK, RUN]),
-                    op=ALU.mult,
-                )
+                scale_columns(nc.gpsimd, l, c, VECTOR_COLS, OUT, inv_gpsimd[:], nd)
+                scale_columns(nc.vector, l, c, 0, VECTOR_COLS, inv_rows[:, :VECTOR_COLS], nd)
             for c in range(PASSES):
                 nc.vector.quantize_mx(
                     out=codes[:, c, :].bitcast(FP8X4),
@@ -165,10 +169,8 @@ def tile_npertokenswishglu_basis_pb_kernel(tc, h, w_down_mix, out):
                 y_tiles.append(y)
             row_inv = inverse_norm(row_sq, B_TILES, "row")
             unit = result.tile([P, B_TILES, OUT], F32, name="unit")
-            for i in range(B_TILES):
-                nc.scalar.activation(
-                    out=unit[:, i, :], in_=y_tiles[i][:], func=ACT.Copy, scale=row_inv[:, i : i + 1]
-                )
+            nc.scalar.activation(out=unit[:, 0, :], in_=y_tiles[0][:], func=ACT.Copy, scale=row_inv[:, 0:1])
+            nc.vector.tensor_scalar_mul(out=unit[:, 1, :], in0=y_tiles[1][:], scalar1=row_inv[:, 1:2])
             nc.sync.dma_start(out=out.rearrange("(i p) l j -> p i l j", p=P)[:, :, l, :], in_=unit[:])
 
         NORMS_AHEAD = 1

@@ -89,15 +89,18 @@ def tile_npertokenswishglu_basis_pb_kernel(tc, h, w_down_mix, out):
                     accum_out=col_sq[:, m : m + 1],
                 )
             col_inv = inverse_norm(col_sq, J_BLOCKS, "col")
+            repeated = work.tile([P, J_BLOCKS, P], F32, name="repeated")
+            nc.gpsimd.tensor_scalar(
+                out=repeated[:],
+                in0=col_inv[:].unsqueeze(2).to_broadcast([P, J_BLOCKS, P]),
+                scalar1=1.0,
+                scalar2=0.0,
+                op0=ALU.mult,
+                op1=ALU.add,
+            )
             inv_rows = inv_psum.tile([P, OUT], F32, name="inv_rows")
             for m in range(J_BLOCKS):
-                nc.tensor.matmul(
-                    out=inv_rows[:, m * P : (m + 1) * P],
-                    lhsT=col_inv[:, m : m + 1].to_broadcast([P, P]),
-                    rhs=ident_f32[:],
-                    start=True,
-                    stop=True,
-                )
+                nc.tensor.transpose(inv_rows[:, m * P : (m + 1) * P], repeated[:, m, :], ident_f32[:])
             return inv_rows
 
         def scale_columns(engine, l, c, first, last, inv, nd):

@@ -13,15 +13,16 @@ ALU = mybir.AluOpType
 
 P = 128
 PACK = 4
+PAIR = 2
+WORDS = PACK // PAIR
 BATCH, TOKENS, HIDDEN, OUT = 256, 8, 1024, 512
 PASSES = HIDDEN // (P * PACK)
 ROWS = PASSES * PACK
-HALVES = 2
 B_TILES = BATCH // P
 J_BLOCKS = OUT // P
 EPS = 1e-12
 TOKENS_PER_H_LOAD = 2
-VECTOR_COLS = 320
+VECTOR_COLS = 352
 RUN = 4
 
 FLOPS = 2 * BATCH * TOKENS * HIDDEN * OUT
@@ -34,14 +35,14 @@ def tile_npertokenswishglu_basis_pb_kernel(tc, h, w_down_mix, out):
         w_pool = stack.enter_context(tc.tile_pool(name="w_pool", bufs=TOKENS))
         h_pool = stack.enter_context(tc.tile_pool(name="h_pool", bufs=TOKENS // TOKENS_PER_H_LOAD))
         h_mx = stack.enter_context(tc.tile_pool(name="h_mx", bufs=TOKENS))
-        work = stack.enter_context(tc.tile_pool(name="work", bufs=2))
-        unread = stack.enter_context(tc.tile_pool(name="unread", bufs=4))
-        small = stack.enter_context(tc.tile_pool(name="small", bufs=4))
+        work = stack.enter_context(tc.tile_pool(name="work", bufs=3))
         result = stack.enter_context(tc.tile_pool(name="result", bufs=3))
+        small = stack.enter_context(tc.tile_pool(name="small", bufs=4))
+        unread = stack.enter_context(tc.tile_pool(name="unread", bufs=4))
         wT_psum = stack.enter_context(tc.psum_pool(name="wT_psum", bufs=3))
         inv_psum = stack.enter_context(tc.psum_pool(name="inv_psum", bufs=2))
         hT_psum = stack.enter_context(tc.psum_pool(name="hT_psum", bufs=1))
-        y_psum = stack.enter_context(tc.psum_pool(name="y_psum", bufs=2))
+        y_psum = stack.enter_context(tc.psum_pool(name="y_psum", bufs=B_TILES))
 
         w_sb = []
         h_sb = []
@@ -49,14 +50,16 @@ def tile_npertokenswishglu_basis_pb_kernel(tc, h, w_down_mix, out):
         for l in range(TOKENS):
             w_tile = w_pool.tile([P, ROWS, OUT], BF16, name="w_tile")
             nc.sync.dma_start(
-                out=w_tile[:].rearrange("p (g e) j -> p g (e j)", e=2),
-                in_=w_down_mix[l].rearrange("(g p e) j -> p g (e j)", p=P, e=2),
+                out=w_tile[:].rearrange("p (g e) j -> p g (e j)", e=PAIR),
+                in_=w_down_mix[l].rearrange("(g p e) j -> p g (e j)", p=P, e=PAIR),
             )
             w_sb.append(w_tile)
             if l < TOKENS // TOKENS_PER_H_LOAD:
                 h_tile = h_pool.tile([P, B_TILES, TOKENS_PER_H_LOAD, HIDDEN], BF16, name="h_tile")
-                first = l * TOKENS_PER_H_LOAD
-                nc.sync.dma_start(out=h_tile[:], in_=h_view[:, :, first : first + TOKENS_PER_H_LOAD, :])
+                first_token = l * TOKENS_PER_H_LOAD
+                nc.sync.dma_start(
+                    out=h_tile[:], in_=h_view[:, :, first_token : first_token + TOKENS_PER_H_LOAD, :]
+                )
                 h_sb.append(h_tile)
 
         ident_bf = const.tile([P, P], BF16, name="ident_bf")
@@ -71,9 +74,11 @@ def tile_npertokenswishglu_basis_pb_kernel(tc, h, w_down_mix, out):
         def inverse_norm(sum_sq, width, name):
             excess = small.tile([P, width], F32, name=name + "_excess")
             nc.scalar.activation(out=excess[:], in_=sum_sq[:], func=ACT.Relu, bias=-EPS * EPS)
-            inv = small.tile([P, width], F32, name=name + "_inv")
-            nc.scalar.activation(out=inv[:], in_=excess[:], func=ACT.Abs_reciprocal_sqrt, bias=EPS * EPS)
-            return inv
+            inverse = small.tile([P, width], F32, name=name + "_inverse")
+            nc.scalar.activation(
+                out=inverse[:], in_=excess[:], func=ACT.Abs_reciprocal_sqrt, bias=EPS * EPS
+            )
+            return inverse
 
         def weight_norms(l):
             col_sq = small.tile([P, J_BLOCKS], F32, name="col_sq")
@@ -89,63 +94,68 @@ def tile_npertokenswishglu_basis_pb_kernel(tc, h, w_down_mix, out):
                     accum_out=col_sq[:, m : m + 1],
                 )
             col_inv = inverse_norm(col_sq, J_BLOCKS, "col")
-            repeated = work.tile([P, J_BLOCKS, P], F32, name="repeated")
-            nc.gpsimd.tensor_scalar(
-                out=repeated[:],
-                in0=col_inv[:].unsqueeze(2).to_broadcast([P, J_BLOCKS, P]),
-                scalar1=1.0,
-                scalar2=0.0,
-                op0=ALU.mult,
-                op1=ALU.add,
-            )
             inv_rows = inv_psum.tile([P, OUT], F32, name="inv_rows")
             for m in range(J_BLOCKS):
-                nc.tensor.transpose(inv_rows[:, m * P : (m + 1) * P], repeated[:, m, :], ident_f32[:])
+                nc.tensor.matmul(
+                    out=inv_rows[:, m * P : (m + 1) * P],
+                    lhsT=col_inv[:, m : m + 1].to_broadcast([P, P]),
+                    rhs=ident_f32[:],
+                    start=True,
+                    stop=True,
+                )
             return inv_rows
 
-        def scale_columns(engine, l, c, first, last, inv, nd):
+        def scale_columns(engine, l, c, first_col, last_col, inv, nd):
             engine.tensor_tensor(
-                out=nd[:, c, first:last, :].rearrange("p (n i) t -> p n t i", i=RUN),
-                in0=w_sb[l][:, c * PACK : (c + 1) * PACK, first:last].rearrange("p t (n i) -> p n t i", i=RUN),
+                out=nd[:, c, first_col:last_col, :].rearrange("p (n i) t -> p n t i", i=RUN),
+                in0=w_sb[l][:, c * PACK : (c + 1) * PACK, first_col:last_col].rearrange(
+                    "p t (n i) -> p n t i", i=RUN
+                ),
                 in1=inv.rearrange("p (n i) -> p n i", i=RUN)
                 .unsqueeze(2)
-                .to_broadcast([P, (last - first) // RUN, PACK, RUN]),
+                .to_broadcast([P, (last_col - first_col) // RUN, PACK, RUN]),
                 op=ALU.mult,
             )
 
-        def quantise_weight(l, inv_rows):
+        def scale_on_gpsimd(l, inv_rows):
             nd = work.tile([P, PASSES, OUT, PACK], BF16, name="nd", align_bytes=64)
-            codes = work.tile([P, PASSES, OUT], U32, name="w_codes", align_bytes=64)
-            scales = work.tile([P, PASSES, OUT], U8, name="w_scales", align_bytes=64)
             inv_gpsimd = work.tile([P, OUT - VECTOR_COLS], F32, name="inv_gpsimd")
             nc.vector.tensor_copy(out=inv_gpsimd[:], in_=inv_rows[:, VECTOR_COLS:])
             for c in range(PASSES):
                 scale_columns(nc.gpsimd, l, c, VECTOR_COLS, OUT, inv_gpsimd[:], nd)
+            return nd
+
+        def quantise_weight(l, inv_rows, nd):
+            w_codes = work.tile([P, PASSES, OUT], U32, name="w_codes", align_bytes=64)
+            w_scales = work.tile([P, PASSES, OUT], U8, name="w_scales", align_bytes=64)
+            for c in range(PASSES):
                 scale_columns(nc.vector, l, c, 0, VECTOR_COLS, inv_rows[:, :VECTOR_COLS], nd)
             for c in range(PASSES):
                 nc.vector.quantize_mx(
-                    out=codes[:, c, :].bitcast(FP8X4),
-                    scales=scales[:, c, :],
+                    out=w_codes[:, c, :].bitcast(FP8X4),
+                    scales=w_scales[:, c, :],
                     in_=nd[:, c].rearrange("p j t -> p (j t)"),
                 )
-            return codes, scales
+            return w_codes, w_scales
 
         def quantise_hidden(l):
             h_tile = h_sb[l // TOKENS_PER_H_LOAD]
             grouped = work.tile([P, PASSES * BATCH * PACK], BF16, name="h_grouped", align_bytes=64)
-            grouped_words = grouped[:].bitcast(F32).rearrange("p (c b u) -> p c b u", c=PASSES, u=HALVES)
+            grouped_words = grouped[:].bitcast(F32).rearrange("p (c b u) -> p c b u", c=PASSES, u=WORDS)
             for c in range(PASSES):
-                hT = hT_psum.tile([P, HALVES, B_TILES, P], F32, name="hT")
-                for u in range(HALVES):
+                hT = hT_psum.tile([P, WORDS, B_TILES, P], F32, name="hT")
+                for u in range(WORDS):
                     for i in range(B_TILES):
-                        words = h_tile[:, i, l % TOKENS_PER_H_LOAD, :].bitcast(F32)
-                        first = (c * HALVES + u) * P
-                        nc.tensor.transpose(hT[:, u, i, :], words[:, first : first + P], ident_f32[:])
+                        h_words = h_tile[:, i, l % TOKENS_PER_H_LOAD, :].bitcast(F32)
+                        first_word = (c * WORDS + u) * P
+                        nc.tensor.transpose(
+                            hT[:, u, i, :], h_words[:, first_word : first_word + P], ident_f32[:]
+                        )
                 nc.vector.tensor_copy(out=grouped_words[:, c], in_=hT[:].rearrange("p u i b -> p (i b) u"))
-            codes = h_mx.tile([P, PASSES * BATCH], U32, name="h_codes", align_bytes=64)
-            scales = h_mx.tile([P, PASSES * BATCH], U8, name="h_scales", align_bytes=64)
-            nc.vector.quantize_mx(out=codes[:].bitcast(FP8X4), scales=scales[:], in_=grouped[:])
-            return codes, scales
+            h_codes = h_mx.tile([P, PASSES * BATCH], U32, name="h_codes", align_bytes=64)
+            h_scales = h_mx.tile([P, PASSES * BATCH], U8, name="h_scales", align_bytes=64)
+            nc.vector.quantize_mx(out=h_codes[:].bitcast(FP8X4), scales=h_scales[:], in_=grouped[:])
+            return h_codes, h_scales
 
         def project(l, h_q, w_q):
             h_codes, h_scales = h_q
@@ -176,18 +186,18 @@ def tile_npertokenswishglu_basis_pb_kernel(tc, h, w_down_mix, out):
             nc.vector.tensor_scalar_mul(out=unit[:, 1, :], in0=y_tiles[1][:], scalar1=row_inv[:, 1:2])
             nc.sync.dma_start(out=out.rearrange("(i p) l j -> p i l j", p=P)[:, :, l, :], in_=unit[:])
 
-        NORMS_AHEAD = 1
         HIDDEN_AHEAD = 2
-        inv_rows = {}
         h_q = {}
-        for l in range(NORMS_AHEAD):
-            inv_rows[l] = weight_norms(l)
+        inv_next = weight_norms(0)
+        nd_next = scale_on_gpsimd(0, inv_next)
         for l in range(HIDDEN_AHEAD):
             h_q[l] = quantise_hidden(l)
         for l in range(TOKENS):
-            if l + NORMS_AHEAD < TOKENS:
-                inv_rows[l + NORMS_AHEAD] = weight_norms(l + NORMS_AHEAD)
+            inv_now, nd_now = inv_next, nd_next
+            if l + 1 < TOKENS:
+                inv_next = weight_norms(l + 1)
+                nd_next = scale_on_gpsimd(l + 1, inv_next)
             if l + HIDDEN_AHEAD < TOKENS:
                 h_q[l + HIDDEN_AHEAD] = quantise_hidden(l + HIDDEN_AHEAD)
-            w_q = quantise_weight(l, inv_rows[l])
+            w_q = quantise_weight(l, inv_now, nd_now)
             project(l, h_q[l], w_q)

from contextlib import ExitStack

import concourse.mybir as mybir
from concourse.masks import make_identity

BF16 = mybir.dt.bfloat16
F32 = mybir.dt.float32
U32 = mybir.dt.uint32
U8 = mybir.dt.uint8
FP8X4 = mybir.dt.float8_e4m3fn_x4
ACT = mybir.ActivationFunctionType
ALU = mybir.AluOpType

P = 128
PACK = 4
PAIR = 2
WORDS = PACK // PAIR
BATCH, TOKENS, HIDDEN, OUT = 256, 8, 1024, 512
PASSES = HIDDEN // (P * PACK)
ROWS = PASSES * PACK
B_TILES = BATCH // P
J_BLOCKS = OUT // P
EPS = 1e-12
TOKENS_PER_H_LOAD = 2
VECTOR_COLS = 352
RUN = 4

FLOPS = 2 * BATCH * TOKENS * HIDDEN * OUT


def tile_npertokenswishglu_basis_pb_kernel(tc, h, w_down_mix, out):
    nc = tc.nc
    with ExitStack() as stack:
        const = stack.enter_context(tc.tile_pool(name="const", bufs=1))
        w_pool = stack.enter_context(tc.tile_pool(name="w_pool", bufs=TOKENS))
        h_pool = stack.enter_context(tc.tile_pool(name="h_pool", bufs=TOKENS // TOKENS_PER_H_LOAD))
        h_mx = stack.enter_context(tc.tile_pool(name="h_mx", bufs=TOKENS))
        work = stack.enter_context(tc.tile_pool(name="work", bufs=3))
        result = stack.enter_context(tc.tile_pool(name="result", bufs=3))
        small = stack.enter_context(tc.tile_pool(name="small", bufs=4))
        unread = stack.enter_context(tc.tile_pool(name="unread", bufs=4))
        wT_psum = stack.enter_context(tc.psum_pool(name="wT_psum", bufs=3))
        inv_psum = stack.enter_context(tc.psum_pool(name="inv_psum", bufs=2))
        hT_psum = stack.enter_context(tc.psum_pool(name="hT_psum", bufs=1))
        y_psum = stack.enter_context(tc.psum_pool(name="y_psum", bufs=B_TILES))

        w_sb = []
        h_sb = []
        h_view = h.rearrange("(i p) l f -> p i l f", p=P)
        for l in range(TOKENS):
            w_tile = w_pool.tile([P, ROWS, OUT], BF16, name="w_tile")
            nc.sync.dma_start(
                out=w_tile[:].rearrange("p (g e) j -> p g (e j)", e=PAIR),
                in_=w_down_mix[l].rearrange("(g p e) j -> p g (e j)", p=P, e=PAIR),
            )
            w_sb.append(w_tile)
            if l < TOKENS // TOKENS_PER_H_LOAD:
                h_tile = h_pool.tile([P, B_TILES, TOKENS_PER_H_LOAD, HIDDEN], BF16, name="h_tile")
                first_token = l * TOKENS_PER_H_LOAD
                nc.sync.dma_start(
                    out=h_tile[:], in_=h_view[:, :, first_token : first_token + TOKENS_PER_H_LOAD, :]
                )
                h_sb.append(h_tile)

        ident_bf = const.tile([P, P], BF16, name="ident_bf")
        make_identity(nc, ident_bf[:])
        ident_f32 = const.tile([P, P], F32, name="ident_f32")
        make_identity(nc, ident_f32[:])

        one = const.tile([P, 1], F32, name="one")
        nc.vector.memset(one[:], 1.0)
        nc.scalar.activation(out=one[:], in_=one[:], func=ACT.Abs_reciprocal_sqrt)

        def inverse_norm(sum_sq, width, name):
            excess = small.tile([P, width], F32, name=name + "_excess")
            nc.scalar.activation(out=excess[:], in_=sum_sq[:], func=ACT.Relu, bias=-EPS * EPS)
            inverse = small.tile([P, width], F32, name=name + "_inverse")
            nc.scalar.activation(
                out=inverse[:], in_=excess[:], func=ACT.Abs_reciprocal_sqrt, bias=EPS * EPS
            )
            return inverse

        def weight_norms(l):
            col_sq = small.tile([P, J_BLOCKS], F32, name="col_sq")
            for m in range(J_BLOCKS):
                wT = wT_psum.tile([P, ROWS, P], BF16, name="wT")
                for r in range(ROWS):
                    nc.tensor.transpose(wT[:, r, :], w_sb[l][:, r, m * P : (m + 1) * P], ident_bf[:])
                squares = unread.tile([P, ROWS * P], BF16, name="squares")
                nc.scalar.activation(
                    out=squares[:],
                    in_=wT[:].rearrange("p r f -> p (r f)"),
                    func=ACT.Square,
                    accum_out=col_sq[:, m : m + 1],
                )
            col_inv = inverse_norm(col_sq, J_BLOCKS, "col")
            inv_rows = inv_psum.tile([P, OUT], F32, name="inv_rows")
            for m in range(J_BLOCKS):
                nc.tensor.matmul(
                    out=inv_rows[:, m * P : (m + 1) * P],
                    lhsT=col_inv[:, m : m + 1].to_broadcast([P, P]),
                    rhs=ident_f32[:],
                    start=True,
                    stop=True,
                )
            return inv_rows

        def scale_columns(engine, l, c, first_col, last_col, inv, nd):
            engine.tensor_tensor(
                out=nd[:, c, first_col:last_col, :].rearrange("p (n i) t -> p n t i", i=RUN),
                in0=w_sb[l][:, c * PACK : (c + 1) * PACK, first_col:last_col].rearrange(
                    "p t (n i) -> p n t i", i=RUN
                ),
                in1=inv.rearrange("p (n i) -> p n i", i=RUN)
                .unsqueeze(2)
                .to_broadcast([P, (last_col - first_col) // RUN, PACK, RUN]),
                op=ALU.mult,
            )

        def scale_on_gpsimd(l, inv_rows):
            nd = work.tile([P, PASSES, OUT, PACK], BF16, name="nd", align_bytes=64)
            inv_gpsimd = work.tile([P, OUT - VECTOR_COLS], F32, name="inv_gpsimd")
            nc.vector.tensor_copy(out=inv_gpsimd[:], in_=inv_rows[:, VECTOR_COLS:])
            for c in range(PASSES):
                scale_columns(nc.gpsimd, l, c, VECTOR_COLS, OUT, inv_gpsimd[:], nd)
            return nd

        def quantise_weight(l, inv_rows, nd):
            w_codes = work.tile([P, PASSES, OUT], U32, name="w_codes", align_bytes=64)
            w_scales = work.tile([P, PASSES, OUT], U8, name="w_scales", align_bytes=64)
            for c in range(PASSES):
                scale_columns(nc.vector, l, c, 0, VECTOR_COLS, inv_rows[:, :VECTOR_COLS], nd)
            for c in range(PASSES):
                nc.vector.quantize_mx(
                    out=w_codes[:, c, :].bitcast(FP8X4),
                    scales=w_scales[:, c, :],
                    in_=nd[:, c].rearrange("p j t -> p (j t)"),
                )
            return w_codes, w_scales

        def quantise_hidden(l):
            h_tile = h_sb[l // TOKENS_PER_H_LOAD]
            grouped = work.tile([P, PASSES * BATCH * PACK], BF16, name="h_grouped", align_bytes=64)
            grouped_words = grouped[:].bitcast(F32).rearrange("p (c b u) -> p c b u", c=PASSES, u=WORDS)
            for c in range(PASSES):
                hT = hT_psum.tile([P, WORDS, B_TILES, P], F32, name="hT")
                for u in range(WORDS):
                    for i in range(B_TILES):
                        h_words = h_tile[:, i, l % TOKENS_PER_H_LOAD, :].bitcast(F32)
                        first_word = (c * WORDS + u) * P
                        nc.tensor.transpose(
                            hT[:, u, i, :], h_words[:, first_word : first_word + P], ident_f32[:]
                        )
                nc.vector.tensor_copy(out=grouped_words[:, c], in_=hT[:].rearrange("p u i b -> p (i b) u"))
            h_codes = h_mx.tile([P, PASSES * BATCH], U32, name="h_codes", align_bytes=64)
            h_scales = h_mx.tile([P, PASSES * BATCH], U8, name="h_scales", align_bytes=64)
            nc.vector.quantize_mx(out=h_codes[:].bitcast(FP8X4), scales=h_scales[:], in_=grouped[:])
            return h_codes, h_scales

        def project(l, h_q, w_q):
            h_codes, h_scales = h_q
            w_codes, w_scales = w_q
            row_sq = small.tile([P, B_TILES], F32, name="row_sq")
            y_tiles = []
            for i in range(B_TILES):
                y = y_psum.tile([P, OUT], F32, name="y")
                for c in range(PASSES):
                    b_cols = slice((c * B_TILES + i) * P, (c * B_TILES + i + 1) * P)
                    nc.tensor.matmul_mx(
                        out=y[:],
                        lhsT=h_codes[:, b_cols].bitcast(FP8X4),
                        lhsT_scale=h_scales[:, b_cols],
                        rhs=w_codes[:, c, :].bitcast(FP8X4),
                        rhs_scale=w_scales[:, c, :],
                        start=(c == 0),
                        stop=(c == PASSES - 1),
                    )
                y_squares = unread.tile([P, OUT], BF16, name="y_squares")
                nc.scalar.activation(
                    out=y_squares[:], in_=y[:], func=ACT.Square, accum_out=row_sq[:, i : i + 1]
                )
                y_tiles.append(y)
            row_inv = inverse_norm(row_sq, B_TILES, "row")
            unit = result.tile([P, B_TILES, OUT], F32, name="unit")
            nc.scalar.activation(out=unit[:, 0, :], in_=y_tiles[0][:], func=ACT.Copy, scale=row_inv[:, 0:1])
            nc.vector.tensor_scalar_mul(out=unit[:, 1, :], in0=y_tiles[1][:], scalar1=row_inv[:, 1:2])
            nc.sync.dma_start(out=out.rearrange("(i p) l j -> p i l j", p=P)[:, :, l, :], in_=unit[:])

        HIDDEN_AHEAD = 2
        h_q = {}
        inv_next = weight_norms(0)
        nd_next = scale_on_gpsimd(0, inv_next)
        for l in range(HIDDEN_AHEAD):
            h_q[l] = quantise_hidden(l)
        for l in range(TOKENS):
            inv_now, nd_now = inv_next, nd_next
            if l + 1 < TOKENS:
                inv_next = weight_norms(l + 1)
                nd_next = scale_on_gpsimd(l + 1, inv_next)
            if l + HIDDEN_AHEAD < TOKENS:
                h_q[l + HIDDEN_AHEAD] = quantise_hidden(l + HIDDEN_AHEAD)
            w_q = quantise_weight(l, inv_now, nd_now)
            project(l, h_q[l], w_q)
